import numpy as np
import ml_dtypes


def mxq(x, axis, fmt="e4m3"):
    dtype, down = {"e4m3": (ml_dtypes.float8_e4m3fn, 7), "e5m2": (ml_dtypes.float8_e5m2, 14)}[fmt]
    v = np.moveaxis(np.asarray(x, np.float32).astype(ml_dtypes.bfloat16).astype(np.float64), axis, -1)
    blocks = v.reshape(v.shape[:-1] + (-1, 32))
    amax = np.abs(blocks).max(-1, keepdims=True)
    byte = np.maximum(np.where(amax > 0, np.frexp(amax)[1] - 1 + 127, 0) - down, 1)
    scale = np.exp2(byte - 127.0)
    codes = (blocks / scale).astype(np.float32).astype(dtype).astype(np.float64)
    return np.moveaxis((codes * scale).reshape(v.shape), -1, axis)


WIDE = False


def mx_kscale(k):
    if not WIDE:
        return np.ones(k)
    levels = np.array([10, -10, 5, -5, 0])
    if k % 512:
        return np.exp2(np.random.permutation(np.resize(levels, k // 32))).repeat(32)
    a = np.empty((k // 512, 16))
    for p in range(k // 512):
        a[p, :8] = np.random.permutation(np.resize(levels, 8))
        for g in range(8):
            far = levels[np.abs(levels - a[p, g]) >= 10]
            a[p, g + 8] = far[np.random.randint(len(far))]
    return np.exp2(a.ravel()).repeat(32)


BF16 = ml_dtypes.bfloat16


def bf(x):
    return np.asarray(x, np.float32).astype(BF16)


def f64(x):
    return np.asarray(x).astype(np.float64)


B, CIN, HID, FREQ, T, H = 1, 512, 512, 4, 512, 8
HD = HID * FREQ // H
EPS = 1e-5


def draw0():
    s = mx_kscale(CIN)
    return {"x": bf(np.random.standard_normal((B, CIN, FREQ, T)) * s[None, :, None, None]),
            "qkv_w": bf(np.random.standard_normal((3 * HID, CIN)) / np.sqrt(CIN) / s[None, :]),
            "qkv_b": bf(np.random.standard_normal(3 * HID) * 0.2),
            "qkv_alpha": bf(0.25 + 0.05 * np.random.standard_normal(1)),
            "qkv_gamma": bf(1.0 + 0.1 * np.random.standard_normal((1, 3 * HID, 1, FREQ))),
            "qkv_beta": bf(0.1 * np.random.standard_normal((1, 3 * HID, 1, FREQ)))}


def core(x, qkv_w, qkv_b, qkv_alpha, qkv_gamma, qkv_beta):
    xt = np.swapaxes(f64(x), -2, -1)
    y = (mxq(f64(qkv_w), 1, "e4m3") @ mxq(xt, 1, "e4m3").reshape(B, CIN, T * FREQ)).reshape(B, 3 * HID, T, FREQ)
    y = y + f64(qkv_b)[None, :, None, None]
    y = np.where(y >= 0, y, f64(qkv_alpha)[0] * y)
    mu = y.mean(axis=(1, 3), keepdims=True)
    var = np.square(y - mu).mean(axis=(1, 3), keepdims=True)
    n = (y - mu) / np.sqrt(var + EPS) * f64(qkv_gamma) + f64(qkv_beta)
    n = np.swapaxes(np.swapaxes(n, 1, 2).reshape(B, T, H, 3 * HD), 1, 2)
    return (np.ascontiguousarray(n[..., :HD]), np.ascontiguousarray(n[..., HD:2 * HD]), np.ascontiguousarray(n[..., 2 * HD:]))


def e4m3fn_bytes(y):
    return np.clip(np.asarray(y, np.float64), -448.0, 448.0).astype(np.float32).astype(ml_dtypes.float8_e4m3fn).view(np.uint8)


def e4m3fn_values(b):
    return np.asarray(b, np.uint8).view(ml_dtypes.float8_e4m3fn).astype(np.float64)


def setup_inputs():
    d = draw0()
    x0 = np.asarray(d['x']).astype(np.float64)
    s = (np.max(np.abs(x0), axis=(0, 2, 3), keepdims=True) / 448.0).astype(np.float32)
    out = {}
    for k, v in d.items():
        if k == 'x':
            out['x_bytes'] = e4m3fn_bytes(x0 / s.astype(np.float64))
            out['x_scale'] = s
        else:
            out[k] = v
    return out


def reference(x_bytes, x_scale, qkv_w, qkv_b, qkv_alpha, qkv_gamma, qkv_beta):
    return core(e4m3fn_values(x_bytes) * x_scale.astype(np.float64), qkv_w, qkv_b, qkv_alpha, qkv_gamma, qkv_beta)

@@ -1,0 +1,366 @@
+from contextlib import ExitStack
+
+import concourse.mybir as mybir
+from concourse.masks import make_identity
+
+F32 = mybir.dt.float32
+BF16 = mybir.dt.bfloat16
+U32 = mybir.dt.uint32
+U8 = mybir.dt.uint8
+FP8 = mybir.dt.float8_e4m3fn
+FP8X4 = mybir.dt.float8_e4m3fn_x4
+ALU = mybir.AluOpType
+ACT = mybir.ActivationFunctionType
+
+P = 128
+PACK = 4
+C_IN = 512
+FREQ = 4
+T = 512
+O = 1536
+EPS = 1e-5
+FLOPS = 2 * O * C_IN * FREQ * T
+
+O_TILES = O // P
+T_TILES = T // P
+NORM = O * FREQ
+BANK = FREQ * P
+BANKS = T_TILES * O_TILES
+W_PAIRS = O_TILES // 2
+
+HEAD_PARTS = 3
+CHUNK_BANKS = 3
+CHUNK_HEADS = 2
+CHUNK_COLS = CHUNK_BANKS * BANK
+CHUNKS = BANKS // CHUNK_BANKS
+T_TILE_CHUNKS = CHUNKS // T_TILES
+
+Y_BUFS = 3
+TURNED_BUFS = 3
+SUM_BUFS = 2
+
+MX_AHEAD = 2
+BIAS_AHEAD = 1
+SUM_LAG = 2
+MEAN_STEP = O_TILES + 1
+TURN_LAG = MEAN_STEP + 1
+GAIN_LAG = TURN_LAG + 1
+STD_STEP = GAIN_LAG + O_TILES
+SHIFT_LAG = STD_STEP + 3
+
+Z_BUFS = BIAS_AHEAD + TURN_LAG + 3
+CHUNK_BUFS = 8
+
+X_INTERLEAVE_AT = {15: 2, 24: 3}
+X_QUANTIZE_AT = {3: 1, 17: 2, 26: 3}
+
+
+def tile_unified2dattentiononframe_pa_kernel(
+    tc, x_bytes, x_scale, qkv_w, qkv_b, qkv_alpha, qkv_gamma, qkv_beta, out_0, out_1, out_2
+):
+    nc = tc.nc
+    outs = (out_0, out_1, out_2)
+
+    with ExitStack() as ctx:
+        const = ctx.enter_context(tc.tile_pool(name="const", bufs=1))
+        work = ctx.enter_context(tc.tile_pool(name="work", bufs=2))
+        psum = ctx.enter_context(tc.psum_pool(name="psum", bufs=2))
+        ctx.enter_context(tc.manual_schedule())
+
+        b_rows = const.tile([P, P], BF16, name="b_rows")
+        nc.vector.memset(b_rows[:], 0.0)
+        ones = const.tile([P, 1], F32, name="ones")
+        nc.vector.memset(ones[:], 1.0)
+
+        alpha_bf = const.tile([P, 1], BF16, name="alpha_bf")
+        nc.sync.dma_start(out=alpha_bf[:], in_=qkv_alpha.partition_broadcast(P))
+        scale_raw = const.tile([P, PACK], F32, name="scale_raw")
+        nc.sync.dma_start(out=scale_raw[:], in_=x_scale[0, :, 0, 0].rearrange("(p j) -> p j", j=PACK))
+        x_codes_in = const.tile([P, PACK, FREQ * T], U8, name="x_codes_in")
+        x_planes = x_bytes[0].rearrange("(p j) f t -> p j (f t)", j=PACK)
+        for j in range(PACK):
+            nc.sync.dma_start(out=x_codes_in[:, j, :], in_=x_planes[:, j, :])
+        nc.sync.dma_start(out=b_rows[0:O_TILES, :], in_=qkv_b.rearrange("(i p) -> i p", p=P))
+
+        w_rows = const.tile([P, O_TILES, C_IN], BF16, name="w_rows")
+        w_view = qkv_w.rearrange("(i p) c -> p i c", p=P)
+        for pair in range(W_PAIRS):
+            nc.sync.dma_start(out=w_rows[:, 2 * pair : 2 * pair + 2, :], in_=w_view[:, 2 * pair : 2 * pair + 2, :])
+
+        gamma_all = const.tile([P, NORM], BF16, name="gamma_all")
+        nc.sync.dma_start(out=gamma_all[:], in_=qkv_gamma[0, :, 0, :].rearrange("o f -> (o f)").partition_broadcast(P))
+        beta_all = const.tile([P, NORM], BF16, name="beta_all")
+        nc.sync.dma_start(out=beta_all[:], in_=qkv_beta[0, :, 0, :].rearrange("o f -> (o f)").partition_broadcast(P))
+
+        warm = const.tile([P, 1], F32, name="warm")
+        nc.scalar.activation(out=warm[:], in_=ones[:], func=ACT.Sqrt)
+        ident_f32 = const.tile([P, P], F32, name="ident_f32")
+        make_identity(nc, ident_f32[:])
+        ident_bf16 = const.tile([P, P], BF16, name="ident_bf16")
+        make_identity(nc, ident_bf16[:])
+
+        slope = const.tile([P, 1], F32, name="slope")
+        nc.vector.tensor_copy(out=slope[:], in_=alpha_bf[:])
+        sign_part = const.tile([P, 1], F32, name="sign_part")
+        nc.vector.tensor_scalar(
+            out=sign_part[:], in0=slope[:], scalar1=1.0, scalar2=-2.0, op0=ALU.is_gt, op1=ALU.mult
+        )
+        sign = const.tile([P, 1], F32, name="sign")
+        nc.vector.tensor_scalar(out=sign[:], in0=sign_part[:], scalar1=1.0, scalar2=None, op0=ALU.add)
+        scale_signed = const.tile([P, PACK], F32, name="scale_signed")
+        nc.vector.tensor_scalar(
+            out=scale_signed[:], in0=scale_raw[:], scalar1=sign[:, 0:1], scalar2=None, op0=ALU.mult
+        )
+
+        b_turned = psum.tile([P, P], BF16, name="b_turned", tag="turned", bufs=TURNED_BUFS)
+        nc.tensor.transpose(b_turned[:], b_rows[:], ident_bf16[:])
+
+        x_wide = const.tile([P, PACK, FREQ, T], BF16, name="x_wide")
+        for j in range(PACK):
+            codes = x_codes_in[:, j, :].bitcast(FP8)
+            plane = x_wide[:, j, :, :].rearrange("p f t -> p (f t)")
+            if j == 0:
+                nc.scalar.activation(out=plane, in_=codes, func=ACT.Copy, scale=scale_signed[:, j : j + 1])
+            else:
+                nc.vector.tensor_scalar(
+                    out=plane, in0=codes, scalar1=scale_signed[:, j : j + 1], scalar2=None, op0=ALU.mult
+                )
+
+        x_mx = const.tile([P, T_TILES * BANK], U32, name="x_mx", align_bytes=64)
+        x_mx_scales = const.tile([P, T_TILES * BANK], U8, name="x_mx_scales", align_bytes=64)
+        x_grouped = {}
+
+        def x_interleave(t_tile):
+            grouped = work.tile([P, BANK * PACK], BF16, name="x_grouped", tag="x_grouped", align_bytes=64)
+            x_grouped[t_tile] = grouped
+            nc.vector.tensor_copy(
+                out=grouped[:].rearrange("p (f t j) -> p f t j", f=FREQ, j=PACK),
+                in_=x_wide[:, :, :, t_tile * P : (t_tile + 1) * P].rearrange("p j f t -> p f t j"),
+            )
+
+        def x_quantize(t_tile):
+            nc.vector.quantize_mx(
+                out=x_mx[:, t_tile * BANK : (t_tile + 1) * BANK].bitcast(FP8X4),
+                scales=x_mx_scales[:, t_tile * BANK : (t_tile + 1) * BANK],
+                in_=x_grouped[t_tile][:],
+            )
+
+        w_grouped = const.tile([P, O * PACK], BF16, name="w_grouped", align_bytes=64)
+        w_mx = const.tile([P, O], U32, name="w_mx", align_bytes=64)
+        w_mx_scales = const.tile([P, O], U8, name="w_mx_scales", align_bytes=64)
+        w_words = w_rows[:].rearrange("p i c -> p (i c)").bitcast(F32)
+        w_grouped_words = w_grouped[:].bitcast(F32).rearrange("p (i o u) -> p i o u", i=O_TILES, u=2)
+        row_words = C_IN // 2
+
+        def w_turn(pair):
+            turned = psum.tile([P, 2, 2, P], F32, name="w_turned", tag="turned", bufs=TURNED_BUFS)
+            for half in range(2):
+                i = 2 * pair + half
+                for u in range(2):
+                    nc.tensor.transpose(
+                        turned[:, half, u, :], w_words[:, row_words * i + u : row_words * (i + 1) : 2], ident_f32[:]
+                    )
+            nc.scalar.copy(
+                out=w_grouped_words[:, 2 * pair : 2 * pair + 2, :, :], in_=turned[:].rearrange("p i u o -> p i o u")
+            )
+
+        def w_quantize(pair):
+            nc.vector.quantize_mx(
+                out=w_mx[:, 2 * pair * P : 2 * (pair + 1) * P].bitcast(FP8X4),
+                scales=w_mx_scales[:, 2 * pair * P : 2 * (pair + 1) * P],
+                in_=w_grouped[:, 2 * pair * P * PACK : 2 * (pair + 1) * P * PACK],
+            )
+
+        for pair in range(W_PAIRS):
+            w_turn(pair)
+        x_interleave(0)
+        w_quantize(0)
+        x_quantize(0)
+        bias_signed = const.tile([P, O_TILES], F32, name="bias_signed")
+        nc.vector.tensor_scalar(
+            out=bias_signed[:], in0=b_turned[:, 0:O_TILES], scalar1=sign[:, 0:1], scalar2=None, op0=ALU.mult
+        )
+        w_quantize(1)
+        x_interleave(1)
+        for pair in range(2, W_PAIRS):
+            w_quantize(pair)
+
+        y_of = {}
+        z_of = {}
+        turned_of = {}
+        chunk_of = {}
+        sum_of = {}
+        neg_mean_of = {}
+        squares_of = {}
+        std_of = {}
+        inv_std_of = {}
+
+        def multiply(bank):
+            t_tile, i = divmod(bank, O_TILES)
+            y = psum.tile([P, BANK], F32, name="y", tag="y", bufs=Y_BUFS)
+            y_of[bank] = y
+            nc.tensor.matmul_mx(
+                out=y[:],
+                lhsT=w_mx[:, i * P : (i + 1) * P].bitcast(FP8X4),
+                lhsT_scale=w_mx_scales[:, i * P : (i + 1) * P],
+                rhs=x_mx[:, t_tile * BANK : (t_tile + 1) * BANK].bitcast(FP8X4),
+                rhs_scale=x_mx_scales[:, t_tile * BANK : (t_tile + 1) * BANK],
+                start=True,
+                stop=True,
+            )
+
+        def add_bias(bank):
+            i = bank % O_TILES
+            z = work.tile([P, BANK], F32, name="z", tag="z", bufs=Z_BUFS)
+            z_of[bank] = z
+            nc.scalar.activation(
+                out=z[:], in_=y_of[bank][:], func=ACT.Identity, bias=bias_signed[:, i : i + 1], scale=1.0
+            )
+
+        def prelu(bank):
+            z = z_of[bank]
+            nc.vector.scalar_tensor_tensor(
+                out=z[:], in0=z[:], scalar=slope[:, 0:1], in1=z[:], op0=ALU.mult, op1=ALU.max
+            )
+
+        def add_to_sum(bank):
+            t_tile, i = divmod(bank, O_TILES)
+            if i == 0:
+                sum_of[t_tile] = psum.tile([P, P], F32, name="sum_t", tag="sum_t", bufs=SUM_BUFS)
+            for f in range(FREQ):
+                nc.tensor.matmul(
+                    out=sum_of[t_tile][:],
+                    lhsT=z_of[bank][:, f * P : (f + 1) * P],
+                    rhs=ident_f32[:],
+                    is_transpose=True,
+                    start=(i == 0 and f == 0),
+                    stop=(i == O_TILES - 1 and f == FREQ - 1),
+                )
+
+        def mean(t_tile):
+            neg_mean = work.tile([P, 1], F32, name="neg_mean", tag="neg_mean", bufs=T_TILES)
+            unused = work.tile([P, P], BF16, name="unused_mean", tag="unused_mean")
+            nc.scalar.activation(
+                out=unused[:], in_=sum_of[t_tile][:], func=ACT.Copy, scale=-1.0 / NORM, accum_out=neg_mean[:, 0:1]
+            )
+            neg_mean_of[t_tile] = neg_mean
+            squares_of[t_tile] = work.tile([P, O_TILES], F32, name="squares", tag="squares", bufs=T_TILES)
+
+        def turn(bank):
+            turned = psum.tile([P, FREQ, P], F32, name="turned", tag="turned", bufs=TURNED_BUFS)
+            turned_of[bank] = turned
+            for f in range(FREQ):
+                nc.tensor.matmul(
+                    out=turned[:, f, :],
+                    lhsT=z_of[bank][:, f * P : (f + 1) * P],
+                    rhs=ident_f32[:],
+                    is_transpose=True,
+                    start=True,
+                    stop=True,
+                )
+
+        def square(bank):
+            t_tile, i = divmod(bank, O_TILES)
+            unused = work.tile([P, BANK], BF16, name="unused_square", tag="unused_square")
+            nc.scalar.activation(
+                out=unused[:],
+                in_=turned_of[bank][:].rearrange("p f o -> p (f o)"),
+                func=ACT.Square,
+                bias=neg_mean_of[t_tile][:, 0:1],
+                scale=1.0,
+                accum_out=squares_of[t_tile][:, i : i + 1],
+            )
+
+        def gain(bank):
+            t_tile, i = divmod(bank, O_TILES)
+            chunk_no, bank_in_chunk = divmod(bank, CHUNK_BANKS)
+            if bank_in_chunk == 0:
+                chunk_of[chunk_no] = work.tile([P, CHUNK_COLS], F32, name="chunk", tag="chunk", bufs=CHUNK_BUFS)
+            nc.vector.scalar_tensor_tensor(
+                out=chunk_of[chunk_no][:, bank_in_chunk * BANK : (bank_in_chunk + 1) * BANK].rearrange(
+                    "p (o f) -> p o f", f=FREQ
+                ),
+                in0=turned_of[bank][:].rearrange("p f o -> p o f"),
+                scalar=neg_mean_of[t_tile][:, 0:1],
+                in1=gamma_all[:, i * BANK : (i + 1) * BANK].rearrange("p (o f) -> p o f", f=FREQ),
+                op0=ALU.add,
+                op1=ALU.mult,
+            )
+
+        def std(t_tile):
+            variance = work.tile([P, 1], F32, name="variance", tag="variance", bufs=T_TILES)
+            unused = work.tile([P, O_TILES], F32, name="unused_std", tag="unused_std")
+            nc.scalar.activation(
+                out=unused[:], in_=squares_of[t_tile][:], func=ACT.Copy, scale=1.0 / NORM, accum_out=variance[:, 0:1]
+            )
+            root = work.tile([P, 1], F32, name="root", tag="root", bufs=T_TILES)
+            nc.scalar.activation(out=root[:], in_=variance[:], func=ACT.Sqrt, bias=EPS, scale=1.0)
+            std_of[t_tile] = work.tile([P, 1], F32, name="std_signed", tag="std_signed", bufs=T_TILES)
+            nc.scalar.activation(out=std_of[t_tile][:], in_=root[:], func=ACT.Copy, scale=sign[:, 0:1])
+
+        def inv_std(t_tile):
+            inv_std_of[t_tile] = work.tile([P, 1], F32, name="inv_std", tag="inv_std", bufs=T_TILES)
+            nc.vector.reciprocal(out=inv_std_of[t_tile][:], in_=std_of[t_tile][:])
+
+        def shift_and_store(chunk_no):
+            t_tile, chunk_in_tile = divmod(chunk_no, T_TILE_CHUNKS)
+            chunk = chunk_of[chunk_no]
+            by_head = chunk[:].rearrange("p (h s d) -> p h s d", h=CHUNK_HEADS, s=HEAD_PARTS)
+            pieces = CHUNK_HEADS if chunk_no == CHUNKS - 1 else 1
+            heads = CHUNK_HEADS // pieces
+            cols = CHUNK_COLS // pieces
+            for piece in range(pieces):
+                first_col = chunk_in_tile * CHUNK_COLS + piece * cols
+                nc.vector.scalar_tensor_tensor(
+                    out=chunk[:, piece * cols : (piece + 1) * cols],
+                    in0=chunk[:, piece * cols : (piece + 1) * cols],
+                    scalar=inv_std_of[t_tile][:, 0:1],
+                    in1=beta_all[:, first_col : first_col + cols],
+                    op0=ALU.mult,
+                    op1=ALU.add,
+                )
+                head_in_chunk = piece * heads
+                head = CHUNK_HEADS * chunk_in_tile + head_in_chunk
+                for part in range(HEAD_PARTS):
+                    nc.sync.dma_start(
+                        out=outs[part][0, head : head + heads, t_tile * P : (t_tile + 1) * P, :].rearrange(
+                            "h t d -> t h d"
+                        ),
+                        in_=by_head[:, head_in_chunk : head_in_chunk + heads, part, :],
+                    )
+
+        def banks(*candidates):
+            return list(filter(lambda bank: 0 <= bank < BANKS, candidates))
+
+        def t_tile_at(step, first):
+            t_tile, rest = divmod(step - first, O_TILES)
+            return [t_tile] if rest == 0 and 0 <= t_tile < T_TILES else []
+
+        for n in range(-MX_AHEAD, CHUNK_BANKS * (CHUNKS - 1) + SHIFT_LAG + 1):
+            if n % 2 == 0:
+                for bank in banks(n + MX_AHEAD, n + MX_AHEAD + 1):
+                    multiply(bank)
+            for bank in banks(n + BIAS_AHEAD):
+                add_bias(bank)
+            for bank in banks(n):
+                prelu(bank)
+            if n % 2 == 0:
+                for bank in banks(n - SUM_LAG, n - SUM_LAG + 1):
+                    add_to_sum(bank)
+                for bank in banks(n - TURN_LAG, n - TURN_LAG + 1):
+                    turn(bank)
+            for bank in banks(n - GAIN_LAG):
+                square(bank)
+                gain(bank)
+            for t_tile in t_tile_at(n, MEAN_STEP):
+                mean(t_tile)
+            for t_tile in t_tile_at(n, STD_STEP):
+                std(t_tile)
+            for t_tile in t_tile_at(n, STD_STEP + 1):
+                inv_std(t_tile)
+            if n >= SHIFT_LAG and (n - SHIFT_LAG) % CHUNK_BANKS == 0:
+                shift_and_store((n - SHIFT_LAG) // CHUNK_BANKS)
+            if n in X_INTERLEAVE_AT:
+                x_interleave(X_INTERLEAVE_AT[n])
+            if n in X_QUANTIZE_AT:
+                x_quantize(X_QUANTIZE_AT[n])

@@ -36,13 +36,12 @@ CHUNKS = BANKS // CHUNK_BANKS
 T_TILE_CHUNKS = CHUNKS // T_TILES
 
 Y_BUFS = 3
-TURNED_BUFS = 3
-SUM_BUFS = 2
+TURNED_BUFS = 4
 
 MX_AHEAD = 2
 BIAS_AHEAD = 1
-SUM_LAG = 2
-MEAN_STEP = O_TILES + 1
+SUM_LAG = 4
+MEAN_STEP = O_TILES + 3
 TURN_LAG = MEAN_STEP + 1
 GAIN_LAG = TURN_LAG + 1
 STD_STEP = GAIN_LAG + O_TILES
@@ -194,6 +193,7 @@ def tile_unified2dattentiononframe_pa_kernel(
         squares_of = {}
         std_of = {}
         inv_std_of = {}
+        sums = psum.tile([P, T_TILES, P], F32, name="sums", tag="sums", bufs=1)
 
         def multiply(bank):
             t_tile, i = divmod(bank, O_TILES)
@@ -226,10 +226,10 @@ def tile_unified2dattentiononframe_pa_kernel(
         def add_to_sum(bank):
             t_tile, i = divmod(bank, O_TILES)
             if i == 0:
-                sum_of[t_tile] = psum.tile([P, P], F32, name="sum_t", tag="sum_t", bufs=SUM_BUFS)
+                sum_of[t_tile] = sums[:, t_tile, :]
             for f in range(FREQ):
                 nc.tensor.matmul(
-                    out=sum_of[t_tile][:],
+                    out=sum_of[t_tile],
                     lhsT=z_of[bank][:, f * P : (f + 1) * P],
                     rhs=ident_f32[:],
                     is_transpose=True,
@@ -241,7 +241,7 @@ def tile_unified2dattentiononframe_pa_kernel(
             neg_mean = work.tile([P, 1], F32, name="neg_mean", tag="neg_mean", bufs=T_TILES)
             unused = work.tile([P, P], BF16, name="unused_mean", tag="unused_mean")
             nc.scalar.activation(
-                out=unused[:], in_=sum_of[t_tile][:], func=ACT.Copy, scale=-1.0 / NORM, accum_out=neg_mean[:, 0:1]
+                out=unused[:], in_=sum_of[t_tile], func=ACT.Copy, scale=-1.0 / NORM, accum_out=neg_mean[:, 0:1]
             )
             neg_mean_of[t_tile] = neg_mean
             squares_of[t_tile] = work.tile([P, O_TILES], F32, name="squares", tag="squares", bufs=T_TILES)

@@ -43,7 +43,7 @@ BIAS_AHEAD = 1
 SUM_LAG = 4
 MEAN_STEP = O_TILES + 3
 TURN_LAG = MEAN_STEP + 1
-GAIN_LAG = TURN_LAG + 1
+GAIN_LAG = TURN_LAG + 2
 STD_STEP = GAIN_LAG + O_TILES
 SHIFT_LAG = STD_STEP + 3
 
@@ -118,7 +118,7 @@ def tile_unified2dattentiononframe_pa_kernel(
         for j in range(PACK):
             codes = x_codes_in[:, j, :].bitcast(FP8)
             plane = x_wide[:, j, :, :].rearrange("p f t -> p (f t)")
-            if j == 0:
+            if j == 1:
                 nc.scalar.activation(out=plane, in_=codes, func=ACT.Copy, scale=scale_signed[:, j : j + 1])
             else:
                 nc.vector.tensor_scalar(

@@ -50,6 +50,7 @@ SHIFT_LAG = STD_STEP + 3
 Z_BUFS = BIAS_AHEAD + TURN_LAG + 3
 CHUNK_BUFS = 8
 
+RUN = 4
 X_INTERLEAVE_AT = {15: 2, 24: 3}
 X_QUANTIZE_AT = {3: 1, 17: 2, 26: 3}
 
@@ -133,8 +134,8 @@ def tile_unified2dattentiononframe_pa_kernel(
             grouped = work.tile([P, BANK * PACK], BF16, name="x_grouped", tag="x_grouped", align_bytes=64)
             x_grouped[t_tile] = grouped
             nc.vector.tensor_copy(
-                out=grouped[:].rearrange("p (f t j) -> p f t j", f=FREQ, j=PACK),
-                in_=x_wide[:, :, :, t_tile * P : (t_tile + 1) * P].rearrange("p j f t -> p f t j"),
+                out=grouped[:].rearrange("p (f c i j) -> p f c j i", f=FREQ, i=RUN, j=PACK),
+                in_=x_wide[:, :, :, t_tile * P : (t_tile + 1) * P].rearrange("p j f (c i) -> p f c j i", i=RUN),
             )
 
         def x_quantize(t_tile):

@@ -47,7 +47,18 @@ GAIN_LAG = TURN_LAG + 2
 STD_STEP = GAIN_LAG + O_TILES
 SHIFT_LAG = STD_STEP + 3
 
-Z_BUFS = BIAS_AHEAD + TURN_LAG + 3
+Z_BUFS = BIAS_AHEAD + TURN_LAG + 6
+SHARED_CHUNKS = (3, 6, 7, 10, 11, 15)
+SHARED_FIRST = 2
+SHARED_COLS = (T_TILE_CHUNKS - SHARED_FIRST) * CHUNK_COLS
+SPLIT = 3
+HALF = P // 2
+ROWS_LAG = STD_STEP + 5
+FINAL_TURN_LAG = SHIFT_LAG + 1
+FINAL_AFFINE_LAG = FINAL_TURN_LAG + 1
+FINAL_LAG = FINAL_AFFINE_LAG + 1
+GP_BUFS = 9
+
 CHUNK_BUFS = 8
 
 RUN = 4
@@ -92,12 +103,23 @@ def tile_unified2dattentiononframe_pa_kernel(
         beta_all = const.tile([P, NORM], BF16, name="beta_all")
         nc.sync.dma_start(out=beta_all[:], in_=qkv_beta[0, :, 0, :].rearrange("o f -> (o f)").partition_broadcast(P))
 
+        affine_rows = const.tile([P, SHARED_COLS], BF16, name="affine_rows")
+        for row, source in ((0, qkv_gamma), (HALF, qkv_beta)):
+            nc.sync.dma_start(
+                out=affine_rows[row : row + HALF, :],
+                in_=source[0, :, 0, :].rearrange("o f -> (o f)")[NORM - SHARED_COLS : NORM].partition_broadcast(HALF),
+            )
+        gamma_cols = const.tile([P, O_TILES, FREQ], BF16, name="gamma_cols")
+        nc.sync.dma_start(out=gamma_cols[:], in_=qkv_gamma[0, :, 0, :].rearrange("(i p) f -> p i f", p=P))
+
         warm = const.tile([P, 1], F32, name="warm")
         nc.scalar.activation(out=warm[:], in_=ones[:], func=ACT.Sqrt)
         ident_f32 = const.tile([P, P], F32, name="ident_f32")
         make_identity(nc, ident_f32[:])
         ident_bf16 = const.tile([P, P], BF16, name="ident_bf16")
         make_identity(nc, ident_bf16[:])
+        parts = const.tile([P, T_TILES, P], BF16, name="parts")
+        nc.gpsimd.memset(parts[:], 0.0)
 
         slope = const.tile([P, 1], F32, name="slope")
         nc.vector.tensor_copy(out=slope[:], in_=alpha_bf[:])
@@ -192,8 +214,11 @@ def tile_unified2dattentiononframe_pa_kernel(
         sum_of = {}
         neg_mean_of = {}
         squares_of = {}
-        std_of = {}
         inv_std_of = {}
+        gained_of = {}
+        stats_of = {}
+        stat_rows_of = {}
+        final_of = {}
         sums = psum.tile([P, T_TILES, P], F32, name="sums", tag="sums", bufs=1)
 
         def multiply(bank):
@@ -239,10 +264,11 @@ def tile_unified2dattentiononframe_pa_kernel(
                 )
 
         def mean(t_tile):
-            neg_mean = work.tile([P, 1], F32, name="neg_mean", tag="neg_mean", bufs=T_TILES)
+            stats_of[t_tile] = work.tile([P, 2], F32, name="stats", tag="stats", bufs=T_TILES)
+            neg_mean = stats_of[t_tile][:, 0:1]
             unused = work.tile([P, P], BF16, name="unused_mean", tag="unused_mean")
             nc.scalar.activation(
-                out=unused[:], in_=sum_of[t_tile], func=ACT.Copy, scale=-1.0 / NORM, accum_out=neg_mean[:, 0:1]
+                out=unused[:], in_=sum_of[t_tile], func=ACT.Copy, scale=-1.0 / NORM, accum_out=neg_mean
             )
             neg_mean_of[t_tile] = neg_mean
             squares_of[t_tile] = work.tile([P, O_TILES], F32, name="squares", tag="squares", bufs=T_TILES)
@@ -267,7 +293,7 @@ def tile_unified2dattentiononframe_pa_kernel(
                 out=unused[:],
                 in_=turned_of[bank][:].rearrange("p f o -> p (f o)"),
                 func=ACT.Square,
-                bias=neg_mean_of[t_tile][:, 0:1],
+                bias=neg_mean_of[t_tile],
                 scale=1.0,
                 accum_out=squares_of[t_tile][:, i : i + 1],
             )
@@ -282,7 +308,7 @@ def tile_unified2dattentiononframe_pa_kernel(
                     "p (o f) -> p o f", f=FREQ
                 ),
                 in0=turned_of[bank][:].rearrange("p f o -> p o f"),
-                scalar=neg_mean_of[t_tile][:, 0:1],
+                scalar=neg_mean_of[t_tile],
                 in1=gamma_all[:, i * BANK : (i + 1) * BANK].rearrange("p (o f) -> p o f", f=FREQ),
                 op0=ALU.add,
                 op1=ALU.mult,
@@ -296,39 +322,104 @@ def tile_unified2dattentiononframe_pa_kernel(
             )
             root = work.tile([P, 1], F32, name="root", tag="root", bufs=T_TILES)
             nc.scalar.activation(out=root[:], in_=variance[:], func=ACT.Sqrt, bias=EPS, scale=1.0)
-            std_of[t_tile] = work.tile([P, 1], F32, name="std_signed", tag="std_signed", bufs=T_TILES)
-            nc.scalar.activation(out=std_of[t_tile][:], in_=root[:], func=ACT.Copy, scale=sign[:, 0:1])
+            nc.scalar.activation(out=stats_of[t_tile][:, 1:2], in_=root[:], func=ACT.Copy, scale=sign[:, 0:1])
 
         def inv_std(t_tile):
             inv_std_of[t_tile] = work.tile([P, 1], F32, name="inv_std", tag="inv_std", bufs=T_TILES)
-            nc.vector.reciprocal(out=inv_std_of[t_tile][:], in_=std_of[t_tile][:])
+            nc.vector.reciprocal(out=inv_std_of[t_tile][:], in_=stats_of[t_tile][:, 1:2])
+
+        def split_stats(t_tile):
+            stats = stats_of[t_tile]
+            part = parts[:, t_tile, :].rearrange("p (s k) -> p k s", k=HALF)
+            rest = work.tile([P, 2], F32, name="rest", tag="rest", bufs=T_TILES)
+            nc.gpsimd.tensor_copy(out=part[:, 0, :], in_=stats[:])
+            nc.gpsimd.tensor_tensor(out=rest[:], in0=stats[:], in1=part[:, 0, :], op=ALU.subtract)
+            nc.gpsimd.tensor_copy(out=part[:, 1, :], in_=rest[:])
+            nc.gpsimd.tensor_tensor(out=part[:, 2, :], in0=rest[:], in1=part[:, 1, :], op=ALU.subtract)
+
+        def rows_of_stats(t_tile):
+            rows_turned = psum.tile([P, P], BF16, name="rows_turned", tag="turned", bufs=TURNED_BUFS)
+            nc.tensor.transpose(rows_turned[:], parts[:, t_tile, :], ident_bf16[:])
+            stat_rows_of[t_tile] = work.tile([P, P], BF16, name="stat_rows", tag="stat_rows", bufs=T_TILES)
+            nc.scalar.copy(out=stat_rows_of[t_tile][:], in_=rows_turned[:])
+
+        def gain_by_rows(bank):
+            i = bank % O_TILES
+            gained = work.tile([P, BANK], F32, name="gained", tag="gained", bufs=GP_BUFS)
+            gained_of[bank] = gained
+            for f in range(FREQ):
+                nc.vector.tensor_scalar(
+                    out=gained[:, f * P : (f + 1) * P],
+                    in0=z_of[bank][:, f * P : (f + 1) * P],
+                    scalar1=gamma_cols[:, i, f : f + 1],
+                    scalar2=None,
+                    op0=ALU.mult,
+                )
+
+        def final_turn(bank):
+            final = psum.tile([P, FREQ, P], F32, name="final", tag="y", bufs=Y_BUFS)
+            final_of[bank] = final
+            for f in range(FREQ):
+                nc.tensor.matmul(
+                    out=final[:, f, :],
+                    lhsT=gained_of[bank][:, f * P : (f + 1) * P],
+                    rhs=ident_f32[:],
+                    is_transpose=True,
+                    start=(f == 0),
+                    stop=False,
+                )
+
+        def final_affine(bank):
+            t_tile, i = divmod(bank, O_TILES)
+            first_col = i * BANK - (NORM - SHARED_COLS)
+            final = final_of[bank]
+            nc.tensor.matmul(
+                out=final[:].rearrange("p f o -> p (f o)"),
+                lhsT=stat_rows_of[t_tile][:],
+                rhs=affine_rows[:, first_col : first_col + BANK].rearrange("p (o f) -> p f o", f=FREQ),
+                start=False,
+                stop=True,
+            )
+
+        def final_scale(bank):
+            t_tile = bank // O_TILES
+            chunk_no, bank_in_chunk = divmod(bank, CHUNK_BANKS)
+            if bank_in_chunk == 0:
+                chunk_of[chunk_no] = work.tile([P, CHUNK_COLS], F32, name="chunk", tag="chunk", bufs=CHUNK_BUFS)
+            nc.scalar.activation(
+                out=chunk_of[chunk_no][:, bank_in_chunk * BANK : (bank_in_chunk + 1) * BANK].rearrange(
+                    "p (o f) -> p o f", f=FREQ
+                ),
+                in_=final_of[bank][:].rearrange("p f o -> p o f"),
+                func=ACT.Copy,
+                scale=inv_std_of[t_tile][:, 0:1],
+            )
+
+        def store(chunk_no, head_in_chunk, heads):
+            t_tile, chunk_in_tile = divmod(chunk_no, T_TILE_CHUNKS)
+            by_head = chunk_of[chunk_no][:].rearrange("p (h s d) -> p h s d", h=CHUNK_HEADS, s=HEAD_PARTS)
+            head = CHUNK_HEADS * chunk_in_tile + head_in_chunk
+            for part in range(HEAD_PARTS):
+                nc.sync.dma_start(
+                    out=outs[part][0, head : head + heads, t_tile * P : (t_tile + 1) * P, :].rearrange(
+                        "h t d -> t h d"
+                    ),
+                    in_=by_head[:, head_in_chunk : head_in_chunk + heads, part, :],
+                )
 
         def shift_and_store(chunk_no):
             t_tile, chunk_in_tile = divmod(chunk_no, T_TILE_CHUNKS)
             chunk = chunk_of[chunk_no]
-            by_head = chunk[:].rearrange("p (h s d) -> p h s d", h=CHUNK_HEADS, s=HEAD_PARTS)
-            pieces = CHUNK_HEADS if chunk_no == CHUNKS - 1 else 1
-            heads = CHUNK_HEADS // pieces
-            cols = CHUNK_COLS // pieces
-            for piece in range(pieces):
-                first_col = chunk_in_tile * CHUNK_COLS + piece * cols
-                nc.vector.scalar_tensor_tensor(
-                    out=chunk[:, piece * cols : (piece + 1) * cols],
-                    in0=chunk[:, piece * cols : (piece + 1) * cols],
-                    scalar=inv_std_of[t_tile][:, 0:1],
-                    in1=beta_all[:, first_col : first_col + cols],
-                    op0=ALU.mult,
-                    op1=ALU.add,
-                )
-                head_in_chunk = piece * heads
-                head = CHUNK_HEADS * chunk_in_tile + head_in_chunk
-                for part in range(HEAD_PARTS):
-                    nc.sync.dma_start(
-                        out=outs[part][0, head : head + heads, t_tile * P : (t_tile + 1) * P, :].rearrange(
-                            "h t d -> t h d"
-                        ),
-                        in_=by_head[:, head_in_chunk : head_in_chunk + heads, part, :],
-                    )
+            first_col = chunk_in_tile * CHUNK_COLS
+            nc.vector.scalar_tensor_tensor(
+                out=chunk[:],
+                in0=chunk[:],
+                scalar=inv_std_of[t_tile][:, 0:1],
+                in1=beta_all[:, first_col : first_col + CHUNK_COLS],
+                op0=ALU.mult,
+                op1=ALU.add,
+            )
+            store(chunk_no, 0, CHUNK_HEADS)
 
         def banks(*candidates):
             return list(filter(lambda bank: 0 <= bank < BANKS, candidates))
@@ -337,7 +428,10 @@ def tile_unified2dattentiononframe_pa_kernel(
             t_tile, rest = divmod(step - first, O_TILES)
             return [t_tile] if rest == 0 and 0 <= t_tile < T_TILES else []
 
-        for n in range(-MX_AHEAD, CHUNK_BANKS * (CHUNKS - 1) + SHIFT_LAG + 1):
+        def shared(bank):
+            return bank // CHUNK_BANKS in SHARED_CHUNKS
+
+        for n in range(-MX_AHEAD, BANKS + FINAL_LAG):
             if n % 2 == 0:
                 for bank in banks(n + MX_AHEAD, n + MX_AHEAD + 1):
                     multiply(bank)
@@ -350,17 +444,33 @@ def tile_unified2dattentiononframe_pa_kernel(
                     add_to_sum(bank)
                 for bank in banks(n - TURN_LAG, n - TURN_LAG + 1):
                     turn(bank)
+            for bank in filter(shared, banks(n - FINAL_TURN_LAG)):
+                final_turn(bank)
+            for bank in filter(shared, banks(n - FINAL_AFFINE_LAG)):
+                final_affine(bank)
             for bank in banks(n - GAIN_LAG):
                 square(bank)
-                gain(bank)
+                if shared(bank):
+                    gain_by_rows(bank)
+                else:
+                    gain(bank)
+            for bank in filter(shared, banks(n - FINAL_LAG)):
+                final_scale(bank)
+                if bank % CHUNK_BANKS == CHUNK_BANKS - 1:
+                    store(bank // CHUNK_BANKS, 0, CHUNK_HEADS)
             for t_tile in t_tile_at(n, MEAN_STEP):
                 mean(t_tile)
             for t_tile in t_tile_at(n, STD_STEP):
                 std(t_tile)
+                split_stats(t_tile)
             for t_tile in t_tile_at(n, STD_STEP + 1):
                 inv_std(t_tile)
+            for t_tile in t_tile_at(n, ROWS_LAG):
+                rows_of_stats(t_tile)
             if n >= SHIFT_LAG and (n - SHIFT_LAG) % CHUNK_BANKS == 0:
-                shift_and_store((n - SHIFT_LAG) // CHUNK_BANKS)
+                chunk_no = (n - SHIFT_LAG) // CHUNK_BANKS
+                if chunk_no < CHUNKS and chunk_no not in SHARED_CHUNKS:
+                    shift_and_store(chunk_no)
             if n in X_INTERLEAVE_AT:
                 x_interleave(X_INTERLEAVE_AT[n])
             if n in X_QUANTIZE_AT:

@@ -357,11 +357,11 @@ def tile_unified2dattentiononframe_pa_kernel(
                 )
 
         def final_turn(bank):
-            final = psum.tile([P, FREQ, P], F32, name="final", tag="y", bufs=Y_BUFS)
+            final = psum.tile([P, P, FREQ], F32, name="final", tag="y", bufs=Y_BUFS)
             final_of[bank] = final
             for f in range(FREQ):
                 nc.tensor.matmul(
-                    out=final[:, f, :],
+                    out=final[:, :, f],
                     lhsT=gained_of[bank][:, f * P : (f + 1) * P],
                     rhs=ident_f32[:],
                     is_transpose=True,
@@ -374,9 +374,9 @@ def tile_unified2dattentiononframe_pa_kernel(
             first_col = i * BANK - (NORM - SHARED_COLS)
             final = final_of[bank]
             nc.tensor.matmul(
-                out=final[:].rearrange("p f o -> p (f o)"),
+                out=final[:].rearrange("p o f -> p (o f)"),
                 lhsT=stat_rows_of[t_tile][:],
-                rhs=affine_rows[:, first_col : first_col + BANK].rearrange("p (o f) -> p f o", f=FREQ),
+                rhs=affine_rows[:, first_col : first_col + BANK],
                 start=False,
                 stop=True,
             )
@@ -387,10 +387,8 @@ def tile_unified2dattentiononframe_pa_kernel(
             if bank_in_chunk == 0:
                 chunk_of[chunk_no] = work.tile([P, CHUNK_COLS], F32, name="chunk", tag="chunk", bufs=CHUNK_BUFS)
             nc.scalar.activation(
-                out=chunk_of[chunk_no][:, bank_in_chunk * BANK : (bank_in_chunk + 1) * BANK].rearrange(
-                    "p (o f) -> p o f", f=FREQ
-                ),
-                in_=final_of[bank][:].rearrange("p f o -> p o f"),
+                out=chunk_of[chunk_no][:, bank_in_chunk * BANK : (bank_in_chunk + 1) * BANK],
+                in_=final_of[bank][:].rearrange("p o f -> p (o f)"),
                 func=ACT.Copy,
                 scale=inv_std_of[t_tile][:, 0:1],
             )

@@ -43,12 +43,12 @@ BIAS_AHEAD = 1
 SUM_LAG = 4
 MEAN_STEP = O_TILES + 3
 TURN_LAG = MEAN_STEP + 1
-GAIN_LAG = TURN_LAG + 2
+GAIN_LAG = TURN_LAG + 1
 STD_STEP = GAIN_LAG + O_TILES
 SHIFT_LAG = STD_STEP + 3
 
 Z_BUFS = BIAS_AHEAD + TURN_LAG + 6
-SHARED_CHUNKS = (3, 6, 7, 10, 11, 15)
+SHARED_CHUNKS = (3, 7, 10, 11, 14, 15)
 SHARED_FIRST = 2
 SHARED_COLS = (T_TILE_CHUNKS - SHARED_FIRST) * CHUNK_COLS
 SPLIT = 3
@@ -454,7 +454,11 @@ def tile_unified2dattentiononframe_pa_kernel(
                     gain(bank)
             for bank in filter(shared, banks(n - FINAL_LAG)):
                 final_scale(bank)
-                if bank % CHUNK_BANKS == CHUNK_BANKS - 1:
+                if bank == BANKS - 2:
+                    store(CHUNKS - 1, 0, 1)
+                elif bank == BANKS - 1:
+                    store(CHUNKS - 1, 1, 1)
+                elif bank % CHUNK_BANKS == CHUNK_BANKS - 1:
                     store(bank // CHUNK_BANKS, 0, CHUNK_HEADS)
             for t_tile in t_tile_at(n, MEAN_STEP):
                 mean(t_tile)

@@ -55,8 +55,7 @@ SPLIT = 3
 HALF = P // 2
 ROWS_LAG = STD_STEP + 5
 FINAL_TURN_LAG = SHIFT_LAG + 1
-FINAL_AFFINE_LAG = FINAL_TURN_LAG + 1
-FINAL_LAG = FINAL_AFFINE_LAG + 1
+COPY_LAG = ROWS_LAG + 1
 GP_BUFS = 9
 
 CHUNK_BUFS = 8
@@ -219,6 +218,7 @@ def tile_unified2dattentiononframe_pa_kernel(
         stats_of = {}
         stat_rows_of = {}
         final_of = {}
+        rows_turned_of = {}
         sums = psum.tile([P, T_TILES, P], F32, name="sums", tag="sums", bufs=1)
 
         def multiply(bank):
@@ -338,10 +338,13 @@ def tile_unified2dattentiononframe_pa_kernel(
             nc.gpsimd.tensor_tensor(out=part[:, 2, :], in0=rest[:], in1=part[:, 1, :], op=ALU.subtract)
 
         def rows_of_stats(t_tile):
-            rows_turned = psum.tile([P, P], BF16, name="rows_turned", tag="turned", bufs=TURNED_BUFS)
+            rows_turned = psum.tile([P, P], BF16, name="rows_turned", tag="y", bufs=Y_BUFS)
+            rows_turned_of[t_tile] = rows_turned
             nc.tensor.transpose(rows_turned[:], parts[:, t_tile, :], ident_bf16[:])
+
+        def copy_rows(t_tile):
             stat_rows_of[t_tile] = work.tile([P, P], BF16, name="stat_rows", tag="stat_rows", bufs=T_TILES)
-            nc.scalar.copy(out=stat_rows_of[t_tile][:], in_=rows_turned[:])
+            nc.scalar.copy(out=stat_rows_of[t_tile][:], in_=rows_turned_of[t_tile][:])
 
         def gain_by_rows(bank):
             i = bank % O_TILES
@@ -426,10 +429,13 @@ def tile_unified2dattentiononframe_pa_kernel(
             t_tile, rest = divmod(step - first, O_TILES)
             return [t_tile] if rest == 0 and 0 <= t_tile < T_TILES else []
 
+        def final_step(bank):
+            return bank + FINAL_TURN_LAG + (2 if bank < O_TILES else 0)
+
         def shared(bank):
             return bank // CHUNK_BANKS in SHARED_CHUNKS
 
-        for n in range(-MX_AHEAD, BANKS + FINAL_LAG):
+        for n in range(-MX_AHEAD, final_step(BANKS) + 2):
             if n % 2 == 0:
                 for bank in banks(n + MX_AHEAD, n + MX_AHEAD + 1):
                     multiply(bank)
@@ -442,17 +448,21 @@ def tile_unified2dattentiononframe_pa_kernel(
                     add_to_sum(bank)
                 for bank in banks(n - TURN_LAG, n - TURN_LAG + 1):
                     turn(bank)
-            for bank in filter(shared, banks(n - FINAL_TURN_LAG)):
-                final_turn(bank)
-            for bank in filter(shared, banks(n - FINAL_AFFINE_LAG)):
-                final_affine(bank)
+            for bank in filter(shared, range(BANKS)):
+                if n == final_step(bank) + 1:
+                    final_affine(bank)
+            for bank in filter(shared, range(BANKS)):
+                if n == final_step(bank):
+                    final_turn(bank)
             for bank in banks(n - GAIN_LAG):
                 square(bank)
                 if shared(bank):
                     gain_by_rows(bank)
                 else:
                     gain(bank)
-            for bank in filter(shared, banks(n - FINAL_LAG)):
+            for bank in filter(shared, range(BANKS)):
+                if n != final_step(bank) + 2:
+                    continue
                 final_scale(bank)
                 if bank == BANKS - 2:
                     store(CHUNKS - 1, 0, 1)
@@ -469,6 +479,8 @@ def tile_unified2dattentiononframe_pa_kernel(
                 inv_std(t_tile)
             for t_tile in t_tile_at(n, ROWS_LAG):
                 rows_of_stats(t_tile)
+            for t_tile in t_tile_at(n, COPY_LAG):
+                copy_rows(t_tile)
             if n >= SHIFT_LAG and (n - SHIFT_LAG) % CHUNK_BANKS == 0:
                 chunk_no = (n - SHIFT_LAG) // CHUNK_BANKS
                 if chunk_no < CHUNKS and chunk_no not in SHARED_CHUNKS:

@@ -40,12 +40,17 @@ TURNED_BUFS = 4
 
 MX_AHEAD = 2
 BIAS_AHEAD = 1
-SUM_LAG = 4
-MEAN_STEP = O_TILES + 3
-TURN_LAG = MEAN_STEP + 1
-GAIN_LAG = TURN_LAG + 1
-STD_STEP = GAIN_LAG + O_TILES
-SHIFT_LAG = STD_STEP + 3
+SUM_LAG_FIRST = 4
+SUM_LAG = 6
+MEAN_STEP_FIRST = O_TILES + 4
+MEAN_STEP = O_TILES + 5
+TURN_LAG = O_TILES + 4
+SQUARE_LAG = TURN_LAG + 2
+GAIN_LAG = SQUARE_LAG + 1
+STD_STEP = SQUARE_LAG + O_TILES
+
+SHIFT_FIRST = STD_STEP + 4
+SHIFT_EVERY = 4
 
 Z_BUFS = BIAS_AHEAD + TURN_LAG + 6
 SHARED_CHUNKS = (3, 7, 10, 11, 14, 15)
@@ -54,8 +59,10 @@ SHARED_COLS = (T_TILE_CHUNKS - SHARED_FIRST) * CHUNK_COLS
 SPLIT = 3
 HALF = P // 2
 ROWS_LAG = STD_STEP + 5
-FINAL_TURN_LAG = SHIFT_LAG + 1
 COPY_LAG = ROWS_LAG + 1
+FINAL_TURN_LAG = GAIN_LAG + 14
+FINAL_AFFINE_LAG = FINAL_TURN_LAG + 1
+FINAL_LAG = FINAL_AFFINE_LAG + 2
 GP_BUFS = 9
 
 CHUNK_BUFS = 8
@@ -206,6 +213,7 @@ def tile_unified2dattentiononframe_pa_kernel(
         for pair in range(2, W_PAIRS):
             w_quantize(pair)
 
+        z_pair_of = {}
         y_of = {}
         z_of = {}
         turned_of = {}
@@ -237,16 +245,19 @@ def tile_unified2dattentiononframe_pa_kernel(
 
         def add_bias(bank):
             i = bank % O_TILES
-            z = work.tile([P, BANK], F32, name="z", tag="z", bufs=Z_BUFS)
+            if bank % 2 == 0:
+                z_pair = work.tile([P, 2 * BANK], F32, name="z", tag="z", bufs=(Z_BUFS + 1) // 2)
+                z_pair_of[bank // 2] = z_pair
+            z = z_pair_of[bank // 2][:, bank % 2 * BANK : (bank % 2 + 1) * BANK]
             z_of[bank] = z
             nc.scalar.activation(
-                out=z[:], in_=y_of[bank][:], func=ACT.Identity, bias=bias_signed[:, i : i + 1], scale=1.0
+                out=z, in_=y_of[bank][:], func=ACT.Identity, bias=bias_signed[:, i : i + 1], scale=1.0
             )
 
-        def prelu(bank):
-            z = z_of[bank]
+        def prelu(pair):
+            z = z_pair_of[pair][:]
             nc.vector.scalar_tensor_tensor(
-                out=z[:], in0=z[:], scalar=slope[:, 0:1], in1=z[:], op0=ALU.mult, op1=ALU.max
+                out=z, in0=z, scalar=slope[:, 0:1], in1=z, op0=ALU.mult, op1=ALU.max
             )
 
         def add_to_sum(bank):
@@ -429,40 +440,54 @@ def tile_unified2dattentiononframe_pa_kernel(
             t_tile, rest = divmod(step - first, O_TILES)
             return [t_tile] if rest == 0 and 0 <= t_tile < T_TILES else []
 
-        def final_step(bank):
-            return bank + FINAL_TURN_LAG + (2 if bank < O_TILES else 0)
+        def pairs(step, lag):
+            return banks(step - lag, step - lag + 1) if (step - lag) % 2 == 0 else []
+
+        def in_tile(t_tile, bank):
+            return bank // O_TILES == t_tile
 
         def shared(bank):
             return bank // CHUNK_BANKS in SHARED_CHUNKS
 
-        for n in range(-MX_AHEAD, final_step(BANKS) + 2):
-            if n % 2 == 0:
-                for bank in banks(n + MX_AHEAD, n + MX_AHEAD + 1):
-                    multiply(bank)
+        def final_banks(step, lag):
+            return [bank for bank in banks(step - lag - 2) if shared(bank) and in_tile(0, bank)] + [
+                bank for bank in banks(step - lag) if shared(bank) and not in_tile(0, bank)
+            ]
+
+        own_chunks = [chunk_no for chunk_no in range(CHUNKS) if chunk_no not in SHARED_CHUNKS]
+
+        def shift_step(chunk_no):
+            ready = STD_STEP + O_TILES * (chunk_no // T_TILE_CHUNKS) + 2
+            return max(ready, SHIFT_FIRST + SHIFT_EVERY * own_chunks.index(chunk_no))
+
+        for n in range(-MX_AHEAD, BANKS + FINAL_LAG):
+            for bank in pairs(n, -MX_AHEAD):
+                multiply(bank)
             for bank in banks(n + BIAS_AHEAD):
                 add_bias(bank)
             for bank in banks(n):
-                prelu(bank)
-            if n % 2 == 0:
-                for bank in banks(n - SUM_LAG, n - SUM_LAG + 1):
+                if bank % 2 == 1:
+                    prelu(bank // 2)
+            for bank in pairs(n, SUM_LAG_FIRST):
+                if in_tile(0, bank):
                     add_to_sum(bank)
-                for bank in banks(n - TURN_LAG, n - TURN_LAG + 1):
-                    turn(bank)
-            for bank in filter(shared, range(BANKS)):
-                if n == final_step(bank) + 1:
-                    final_affine(bank)
-            for bank in filter(shared, range(BANKS)):
-                if n == final_step(bank):
-                    final_turn(bank)
-            for bank in banks(n - GAIN_LAG):
+            for bank in pairs(n, SUM_LAG):
+                if not in_tile(0, bank):
+                    add_to_sum(bank)
+            for bank in pairs(n, TURN_LAG):
+                turn(bank)
+            for bank in final_banks(n, FINAL_AFFINE_LAG):
+                final_affine(bank)
+            for bank in final_banks(n, FINAL_TURN_LAG):
+                final_turn(bank)
+            for bank in banks(n - SQUARE_LAG):
                 square(bank)
+            for bank in banks(n - GAIN_LAG):
                 if shared(bank):
                     gain_by_rows(bank)
                 else:
                     gain(bank)
-            for bank in filter(shared, range(BANKS)):
-                if n != final_step(bank) + 2:
-                    continue
+            for bank in final_banks(n, FINAL_LAG):
                 final_scale(bank)
                 if bank == BANKS - 2:
                     store(CHUNKS - 1, 0, 1)
@@ -470,8 +495,11 @@ def tile_unified2dattentiononframe_pa_kernel(
                     store(CHUNKS - 1, 1, 1)
                 elif bank % CHUNK_BANKS == CHUNK_BANKS - 1:
                     store(bank // CHUNK_BANKS, 0, CHUNK_HEADS)
+            if n == MEAN_STEP_FIRST:
+                mean(0)
             for t_tile in t_tile_at(n, MEAN_STEP):
-                mean(t_tile)
+                if t_tile > 0:
+                    mean(t_tile)
             for t_tile in t_tile_at(n, STD_STEP):
                 std(t_tile)
                 split_stats(t_tile)
@@ -481,9 +509,8 @@ def tile_unified2dattentiononframe_pa_kernel(
                 rows_of_stats(t_tile)
             for t_tile in t_tile_at(n, COPY_LAG):
                 copy_rows(t_tile)
-            if n >= SHIFT_LAG and (n - SHIFT_LAG) % CHUNK_BANKS == 0:
-                chunk_no = (n - SHIFT_LAG) // CHUNK_BANKS
-                if chunk_no < CHUNKS and chunk_no not in SHARED_CHUNKS:
+            for chunk_no in own_chunks:
+                if n == shift_step(chunk_no):
                     shift_and_store(chunk_no)
             if n in X_INTERLEAVE_AT:
                 x_interleave(X_INTERLEAVE_AT[n])

from contextlib import ExitStack

import concourse.mybir as mybir
from concourse.masks import make_identity

F32 = mybir.dt.float32
BF16 = mybir.dt.bfloat16
U32 = mybir.dt.uint32
U8 = mybir.dt.uint8
FP8 = mybir.dt.float8_e4m3fn
FP8X4 = mybir.dt.float8_e4m3fn_x4
ALU = mybir.AluOpType
ACT = mybir.ActivationFunctionType

P = 128
PACK = 4
C_IN = 512
FREQ = 4
T = 512
O = 1536
EPS = 1e-5
FLOPS = 2 * O * C_IN * FREQ * T

O_TILES = O // P
T_TILES = T // P
NORM = O * FREQ
BANK = FREQ * P
BANKS = T_TILES * O_TILES
W_PAIRS = O_TILES // 2

HEAD_PARTS = 3
CHUNK_BANKS = 3
CHUNK_HEADS = 2
CHUNK_COLS = CHUNK_BANKS * BANK
CHUNKS = BANKS // CHUNK_BANKS
T_TILE_CHUNKS = CHUNKS // T_TILES

Y_BUFS = 3
TURNED_BUFS = 4

MX_AHEAD = 2
BIAS_AHEAD = 1
SUM_LAG_FIRST = 4
SUM_LAG = 6
MEAN_STEP_FIRST = O_TILES + 4
MEAN_STEP = O_TILES + 5
TURN_LAG = O_TILES + 4
SQUARE_LAG = TURN_LAG + 2
GAIN_LAG = SQUARE_LAG + 1
STD_STEP = SQUARE_LAG + O_TILES

SHIFT_FIRST = STD_STEP + 4
SHIFT_EVERY = 4

Z_BUFS = BIAS_AHEAD + TURN_LAG + 6
SHARED_CHUNKS = (3, 7, 10, 11, 14, 15)
SHARED_FIRST = 2
SHARED_COLS = (T_TILE_CHUNKS - SHARED_FIRST) * CHUNK_COLS
SPLIT = 3
HALF = P // 2
ROWS_LAG = STD_STEP + 5
COPY_LAG = ROWS_LAG + 1
FINAL_TURN_LAG = GAIN_LAG + 14
FINAL_AFFINE_LAG = FINAL_TURN_LAG + 1
FINAL_LAG = FINAL_AFFINE_LAG + 2
GP_BUFS = 9

CHUNK_BUFS = 8

RUN = 4
X_INTERLEAVE_AT = {15: 2, 24: 3}
X_QUANTIZE_AT = {3: 1, 17: 2, 26: 3}


def tile_unified2dattentiononframe_pa_kernel(
    tc, x_bytes, x_scale, qkv_w, qkv_b, qkv_alpha, qkv_gamma, qkv_beta, out_0, out_1, out_2
):
    nc = tc.nc
    outs = (out_0, out_1, out_2)

    with ExitStack() as ctx:
        const = ctx.enter_context(tc.tile_pool(name="const", bufs=1))
        work = ctx.enter_context(tc.tile_pool(name="work", bufs=2))
        psum = ctx.enter_context(tc.psum_pool(name="psum", bufs=2))
        ctx.enter_context(tc.manual_schedule())

        b_rows = const.tile([P, P], BF16, name="b_rows")
        nc.vector.memset(b_rows[:], 0.0)
        ones = const.tile([P, 1], F32, name="ones")
        nc.vector.memset(ones[:], 1.0)

        alpha_bf = const.tile([P, 1], BF16, name="alpha_bf")
        nc.sync.dma_start(out=alpha_bf[:], in_=qkv_alpha.partition_broadcast(P))
        scale_raw = const.tile([P, PACK], F32, name="scale_raw")
        nc.sync.dma_start(out=scale_raw[:], in_=x_scale[0, :, 0, 0].rearrange("(p j) -> p j", j=PACK))
        x_codes_in = const.tile([P, PACK, FREQ * T], U8, name="x_codes_in")
        x_planes = x_bytes[0].rearrange("(p j) f t -> p j (f t)", j=PACK)
        for j in range(PACK):
            nc.sync.dma_start(out=x_codes_in[:, j, :], in_=x_planes[:, j, :])
        nc.sync.dma_start(out=b_rows[0:O_TILES, :], in_=qkv_b.rearrange("(i p) -> i p", p=P))

        w_rows = const.tile([P, O_TILES, C_IN], BF16, name="w_rows")
        w_view = qkv_w.rearrange("(i p) c -> p i c", p=P)
        for pair in range(W_PAIRS):
            nc.sync.dma_start(out=w_rows[:, 2 * pair : 2 * pair + 2, :], in_=w_view[:, 2 * pair : 2 * pair + 2, :])

        gamma_all = const.tile([P, NORM], BF16, name="gamma_all")
        nc.sync.dma_start(out=gamma_all[:], in_=qkv_gamma[0, :, 0, :].rearrange("o f -> (o f)").partition_broadcast(P))
        beta_all = const.tile([P, NORM], BF16, name="beta_all")
        nc.sync.dma_start(out=beta_all[:], in_=qkv_beta[0, :, 0, :].rearrange("o f -> (o f)").partition_broadcast(P))

        affine_rows = const.tile([P, SHARED_COLS], BF16, name="affine_rows")
        for row, source in ((0, qkv_gamma), (HALF, qkv_beta)):
            nc.sync.dma_start(
                out=affine_rows[row : row + HALF, :],
                in_=source[0, :, 0, :].rearrange("o f -> (o f)")[NORM - SHARED_COLS : NORM].partition_broadcast(HALF),
            )
        gamma_cols = const.tile([P, O_TILES, FREQ], BF16, name="gamma_cols")
        nc.sync.dma_start(out=gamma_cols[:], in_=qkv_gamma[0, :, 0, :].rearrange("(i p) f -> p i f", p=P))

        warm = const.tile([P, 1], F32, name="warm")
        nc.scalar.activation(out=warm[:], in_=ones[:], func=ACT.Sqrt)
        ident_f32 = const.tile([P, P], F32, name="ident_f32")
        make_identity(nc, ident_f32[:])
        ident_bf16 = const.tile([P, P], BF16, name="ident_bf16")
        make_identity(nc, ident_bf16[:])
        parts = const.tile([P, T_TILES, P], BF16, name="parts")
        nc.gpsimd.memset(parts[:], 0.0)

        slope = const.tile([P, 1], F32, name="slope")
        nc.vector.tensor_copy(out=slope[:], in_=alpha_bf[:])
        sign_part = const.tile([P, 1], F32, name="sign_part")
        nc.vector.tensor_scalar(
            out=sign_part[:], in0=slope[:], scalar1=1.0, scalar2=-2.0, op0=ALU.is_gt, op1=ALU.mult
        )
        sign = const.tile([P, 1], F32, name="sign")
        nc.vector.tensor_scalar(out=sign[:], in0=sign_part[:], scalar1=1.0, scalar2=None, op0=ALU.add)
        scale_signed = const.tile([P, PACK], F32, name="scale_signed")
        nc.vector.tensor_scalar(
            out=scale_signed[:], in0=scale_raw[:], scalar1=sign[:, 0:1], scalar2=None, op0=ALU.mult
        )

        b_turned = psum.tile([P, P], BF16, name="b_turned", tag="turned", bufs=TURNED_BUFS)
        nc.tensor.transpose(b_turned[:], b_rows[:], ident_bf16[:])

        x_wide = const.tile([P, PACK, FREQ, T], BF16, name="x_wide")
        for j in range(PACK):
            codes = x_codes_in[:, j, :].bitcast(FP8)
            plane = x_wide[:, j, :, :].rearrange("p f t -> p (f t)")
            if j == 1:
                nc.scalar.activation(out=plane, in_=codes, func=ACT.Copy, scale=scale_signed[:, j : j + 1])
            else:
                nc.vector.tensor_scalar(
                    out=plane, in0=codes, scalar1=scale_signed[:, j : j + 1], scalar2=None, op0=ALU.mult
                )

        x_mx = const.tile([P, T_TILES * BANK], U32, name="x_mx", align_bytes=64)
        x_mx_scales = const.tile([P, T_TILES * BANK], U8, name="x_mx_scales", align_bytes=64)
        x_grouped = {}

        def x_interleave(t_tile):
            grouped = work.tile([P, BANK * PACK], BF16, name="x_grouped", tag="x_grouped", align_bytes=64)
            x_grouped[t_tile] = grouped
            nc.vector.tensor_copy(
                out=grouped[:].rearrange("p (f c i j) -> p f c j i", f=FREQ, i=RUN, j=PACK),
                in_=x_wide[:, :, :, t_tile * P : (t_tile + 1) * P].rearrange("p j f (c i) -> p f c j i", i=RUN),
            )

        def x_quantize(t_tile):
            nc.vector.quantize_mx(
                out=x_mx[:, t_tile * BANK : (t_tile + 1) * BANK].bitcast(FP8X4),
                scales=x_mx_scales[:, t_tile * BANK : (t_tile + 1) * BANK],
                in_=x_grouped[t_tile][:],
            )

        w_grouped = const.tile([P, O * PACK], BF16, name="w_grouped", align_bytes=64)
        w_mx = const.tile([P, O], U32, name="w_mx", align_bytes=64)
        w_mx_scales = const.tile([P, O], U8, name="w_mx_scales", align_bytes=64)
        w_words = w_rows[:].rearrange("p i c -> p (i c)").bitcast(F32)
        w_grouped_words = w_grouped[:].bitcast(F32).rearrange("p (i o u) -> p i o u", i=O_TILES, u=2)
        row_words = C_IN // 2

        def w_turn(pair):
            turned = psum.tile([P, 2, 2, P], F32, name="w_turned", tag="turned", bufs=TURNED_BUFS)
            for half in range(2):
                i = 2 * pair + half
                for u in range(2):
                    nc.tensor.transpose(
                        turned[:, half, u, :], w_words[:, row_words * i + u : row_words * (i + 1) : 2], ident_f32[:]
                    )
            nc.scalar.copy(
                out=w_grouped_words[:, 2 * pair : 2 * pair + 2, :, :], in_=turned[:].rearrange("p i u o -> p i o u")
            )

        def w_quantize(pair):
            nc.vector.quantize_mx(
                out=w_mx[:, 2 * pair * P : 2 * (pair + 1) * P].bitcast(FP8X4),
                scales=w_mx_scales[:, 2 * pair * P : 2 * (pair + 1) * P],
                in_=w_grouped[:, 2 * pair * P * PACK : 2 * (pair + 1) * P * PACK],
            )

        for pair in range(W_PAIRS):
            w_turn(pair)
        x_interleave(0)
        w_quantize(0)
        x_quantize(0)
        bias_signed = const.tile([P, O_TILES], F32, name="bias_signed")
        nc.vector.tensor_scalar(
            out=bias_signed[:], in0=b_turned[:, 0:O_TILES], scalar1=sign[:, 0:1], scalar2=None, op0=ALU.mult
        )
        w_quantize(1)
        x_interleave(1)
        for pair in range(2, W_PAIRS):
            w_quantize(pair)

        z_pair_of = {}
        y_of = {}
        z_of = {}
        turned_of = {}
        chunk_of = {}
        sum_of = {}
        neg_mean_of = {}
        squares_of = {}
        inv_std_of = {}
        gained_of = {}
        stats_of = {}
        stat_rows_of = {}
        final_of = {}
        rows_turned_of = {}
        sums = psum.tile([P, T_TILES, P], F32, name="sums", tag="sums", bufs=1)

        def multiply(bank):
            t_tile, i = divmod(bank, O_TILES)
            y = psum.tile([P, BANK], F32, name="y", tag="y", bufs=Y_BUFS)
            y_of[bank] = y
            nc.tensor.matmul_mx(
                out=y[:],
                lhsT=w_mx[:, i * P : (i + 1) * P].bitcast(FP8X4),
                lhsT_scale=w_mx_scales[:, i * P : (i + 1) * P],
                rhs=x_mx[:, t_tile * BANK : (t_tile + 1) * BANK].bitcast(FP8X4),
                rhs_scale=x_mx_scales[:, t_tile * BANK : (t_tile + 1) * BANK],
                start=True,
                stop=True,
            )

        def add_bias(bank):
            i = bank % O_TILES
            if bank % 2 == 0:
                z_pair = work.tile([P, 2 * BANK], F32, name="z", tag="z", bufs=(Z_BUFS + 1) // 2)
                z_pair_of[bank // 2] = z_pair
            z = z_pair_of[bank // 2][:, bank % 2 * BANK : (bank % 2 + 1) * BANK]
            z_of[bank] = z
            nc.scalar.activation(
                out=z, in_=y_of[bank][:], func=ACT.Identity, bias=bias_signed[:, i : i + 1], scale=1.0
            )

        def prelu(pair):
            z = z_pair_of[pair][:]
            nc.vector.scalar_tensor_tensor(
                out=z, in0=z, scalar=slope[:, 0:1], in1=z, op0=ALU.mult, op1=ALU.max
            )

        def add_to_sum(bank):
            t_tile, i = divmod(bank, O_TILES)
            if i == 0:
                sum_of[t_tile] = sums[:, t_tile, :]
            for f in range(FREQ):
                nc.tensor.matmul(
                    out=sum_of[t_tile],
                    lhsT=z_of[bank][:, f * P : (f + 1) * P],
                    rhs=ident_f32[:],
                    is_transpose=True,
                    start=(i == 0 and f == 0),
                    stop=(i == O_TILES - 1 and f == FREQ - 1),
                )

        def mean(t_tile):
            stats_of[t_tile] = work.tile([P, 2], F32, name="stats", tag="stats", bufs=T_TILES)
            neg_mean = stats_of[t_tile][:, 0:1]
            unused = work.tile([P, P], BF16, name="unused_mean", tag="unused_mean")
            nc.scalar.activation(
                out=unused[:], in_=sum_of[t_tile], func=ACT.Copy, scale=-1.0 / NORM, accum_out=neg_mean
            )
            neg_mean_of[t_tile] = neg_mean
            squares_of[t_tile] = work.tile([P, O_TILES], F32, name="squares", tag="squares", bufs=T_TILES)

        def turn(bank):
            turned = psum.tile([P, FREQ, P], F32, name="turned", tag="turned", bufs=TURNED_BUFS)
            turned_of[bank] = turned
            for f in range(FREQ):
                nc.tensor.matmul(
                    out=turned[:, f, :],
                    lhsT=z_of[bank][:, f * P : (f + 1) * P],
                    rhs=ident_f32[:],
                    is_transpose=True,
                    start=True,
                    stop=True,
                )

        def square(bank):
            t_tile, i = divmod(bank, O_TILES)
            unused = work.tile([P, BANK], BF16, name="unused_square", tag="unused_square")
            nc.scalar.activation(
                out=unused[:],
                in_=turned_of[bank][:].rearrange("p f o -> p (f o)"),
                func=ACT.Square,
                bias=neg_mean_of[t_tile],
                scale=1.0,
                accum_out=squares_of[t_tile][:, i : i + 1],
            )

        def gain(bank):
            t_tile, i = divmod(bank, O_TILES)
            chunk_no, bank_in_chunk = divmod(bank, CHUNK_BANKS)
            if bank_in_chunk == 0:
                chunk_of[chunk_no] = work.tile([P, CHUNK_COLS], F32, name="chunk", tag="chunk", bufs=CHUNK_BUFS)
            nc.vector.scalar_tensor_tensor(
                out=chunk_of[chunk_no][:, bank_in_chunk * BANK : (bank_in_chunk + 1) * BANK].rearrange(
                    "p (o f) -> p o f", f=FREQ
                ),
                in0=turned_of[bank][:].rearrange("p f o -> p o f"),
                scalar=neg_mean_of[t_tile],
                in1=gamma_all[:, i * BANK : (i + 1) * BANK].rearrange("p (o f) -> p o f", f=FREQ),
                op0=ALU.add,
                op1=ALU.mult,
            )

        def std(t_tile):
            variance = work.tile([P, 1], F32, name="variance", tag="variance", bufs=T_TILES)
            unused = work.tile([P, O_TILES], F32, name="unused_std", tag="unused_std")
            nc.scalar.activation(
                out=unused[:], in_=squares_of[t_tile][:], func=ACT.Copy, scale=1.0 / NORM, accum_out=variance[:, 0:1]
            )
            root = work.tile([P, 1], F32, name="root", tag="root", bufs=T_TILES)
            nc.scalar.activation(out=root[:], in_=variance[:], func=ACT.Sqrt, bias=EPS, scale=1.0)
            nc.scalar.activation(out=stats_of[t_tile][:, 1:2], in_=root[:], func=ACT.Copy, scale=sign[:, 0:1])

        def inv_std(t_tile):
            inv_std_of[t_tile] = work.tile([P, 1], F32, name="inv_std", tag="inv_std", bufs=T_TILES)
            nc.vector.reciprocal(out=inv_std_of[t_tile][:], in_=stats_of[t_tile][:, 1:2])

        def split_stats(t_tile):
            stats = stats_of[t_tile]
            part = parts[:, t_tile, :].rearrange("p (s k) -> p k s", k=HALF)
            rest = work.tile([P, 2], F32, name="rest", tag="rest", bufs=T_TILES)
            nc.gpsimd.tensor_copy(out=part[:, 0, :], in_=stats[:])
            nc.gpsimd.tensor_tensor(out=rest[:], in0=stats[:], in1=part[:, 0, :], op=ALU.subtract)
            nc.gpsimd.tensor_copy(out=part[:, 1, :], in_=rest[:])
            nc.gpsimd.tensor_tensor(out=part[:, 2, :], in0=rest[:], in1=part[:, 1, :], op=ALU.subtract)

        def rows_of_stats(t_tile):
            rows_turned = psum.tile([P, P], BF16, name="rows_turned", tag="y", bufs=Y_BUFS)
            rows_turned_of[t_tile] = rows_turned
            nc.tensor.transpose(rows_turned[:], parts[:, t_tile, :], ident_bf16[:])

        def copy_rows(t_tile):
            stat_rows_of[t_tile] = work.tile([P, P], BF16, name="stat_rows", tag="stat_rows", bufs=T_TILES)
            nc.scalar.copy(out=stat_rows_of[t_tile][:], in_=rows_turned_of[t_tile][:])

        def gain_by_rows(bank):
            i = bank % O_TILES
            gained = work.tile([P, BANK], F32, name="gained", tag="gained", bufs=GP_BUFS)
            gained_of[bank] = gained
            for f in range(FREQ):
                nc.vector.tensor_scalar(
                    out=gained[:, f * P : (f + 1) * P],
                    in0=z_of[bank][:, f * P : (f + 1) * P],
                    scalar1=gamma_cols[:, i, f : f + 1],
                    scalar2=None,
                    op0=ALU.mult,
                )

        def final_turn(bank):
            final = psum.tile([P, P, FREQ], F32, name="final", tag="y", bufs=Y_BUFS)
            final_of[bank] = final
            for f in range(FREQ):
                nc.tensor.matmul(
                    out=final[:, :, f],
                    lhsT=gained_of[bank][:, f * P : (f + 1) * P],
                    rhs=ident_f32[:],
                    is_transpose=True,
                    start=(f == 0),
                    stop=False,
                )

        def final_affine(bank):
            t_tile, i = divmod(bank, O_TILES)
            first_col = i * BANK - (NORM - SHARED_COLS)
            final = final_of[bank]
            nc.tensor.matmul(
                out=final[:].rearrange("p o f -> p (o f)"),
                lhsT=stat_rows_of[t_tile][:],
                rhs=affine_rows[:, first_col : first_col + BANK],
                start=False,
                stop=True,
            )

        def final_scale(bank):
            t_tile = bank // O_TILES
            chunk_no, bank_in_chunk = divmod(bank, CHUNK_BANKS)
            if bank_in_chunk == 0:
                chunk_of[chunk_no] = work.tile([P, CHUNK_COLS], F32, name="chunk", tag="chunk", bufs=CHUNK_BUFS)
            nc.scalar.activation(
                out=chunk_of[chunk_no][:, bank_in_chunk * BANK : (bank_in_chunk + 1) * BANK],
                in_=final_of[bank][:].rearrange("p o f -> p (o f)"),
                func=ACT.Copy,
                scale=inv_std_of[t_tile][:, 0:1],
            )

        def store(chunk_no, head_in_chunk, heads):
            t_tile, chunk_in_tile = divmod(chunk_no, T_TILE_CHUNKS)
            by_head = chunk_of[chunk_no][:].rearrange("p (h s d) -> p h s d", h=CHUNK_HEADS, s=HEAD_PARTS)
            head = CHUNK_HEADS * chunk_in_tile + head_in_chunk
            for part in range(HEAD_PARTS):
                nc.sync.dma_start(
                    out=outs[part][0, head : head + heads, t_tile * P : (t_tile + 1) * P, :].rearrange(
                        "h t d -> t h d"
                    ),
                    in_=by_head[:, head_in_chunk : head_in_chunk + heads, part, :],
                )

        def shift_and_store(chunk_no):
            t_tile, chunk_in_tile = divmod(chunk_no, T_TILE_CHUNKS)
            chunk = chunk_of[chunk_no]
            first_col = chunk_in_tile * CHUNK_COLS
            nc.vector.scalar_tensor_tensor(
                out=chunk[:],
                in0=chunk[:],
                scalar=inv_std_of[t_tile][:, 0:1],
                in1=beta_all[:, first_col : first_col + CHUNK_COLS],
                op0=ALU.mult,
                op1=ALU.add,
            )
            store(chunk_no, 0, CHUNK_HEADS)

        def banks(*candidates):
            return list(filter(lambda bank: 0 <= bank < BANKS, candidates))

        def t_tile_at(step, first):
            t_tile, rest = divmod(step - first, O_TILES)
            return [t_tile] if rest == 0 and 0 <= t_tile < T_TILES else []

        def pairs(step, lag):
            return banks(step - lag, step - lag + 1) if (step - lag) % 2 == 0 else []

        def in_tile(t_tile, bank):
            return bank // O_TILES == t_tile

        def shared(bank):
            return bank // CHUNK_BANKS in SHARED_CHUNKS

        def final_banks(step, lag):
            return [bank for bank in banks(step - lag - 2) if shared(bank) and in_tile(0, bank)] + [
                bank for bank in banks(step - lag) if shared(bank) and not in_tile(0, bank)
            ]

        own_chunks = [chunk_no for chunk_no in range(CHUNKS) if chunk_no not in SHARED_CHUNKS]

        def shift_step(chunk_no):
            ready = STD_STEP + O_TILES * (chunk_no // T_TILE_CHUNKS) + 2
            return max(ready, SHIFT_FIRST + SHIFT_EVERY * own_chunks.index(chunk_no))

        for n in range(-MX_AHEAD, BANKS + FINAL_LAG):
            for bank in pairs(n, -MX_AHEAD):
                multiply(bank)
            for bank in banks(n + BIAS_AHEAD):
                add_bias(bank)
            for bank in banks(n):
                if bank % 2 == 1:
                    prelu(bank // 2)
            for bank in pairs(n, SUM_LAG_FIRST):
                if in_tile(0, bank):
                    add_to_sum(bank)
            for bank in pairs(n, SUM_LAG):
                if not in_tile(0, bank):
                    add_to_sum(bank)
            for bank in pairs(n, TURN_LAG):
                turn(bank)
            for bank in final_banks(n, FINAL_AFFINE_LAG):
                final_affine(bank)
            for bank in final_banks(n, FINAL_TURN_LAG):
                final_turn(bank)
            for bank in banks(n - SQUARE_LAG):
                square(bank)
            for bank in banks(n - GAIN_LAG):
                if shared(bank):
                    gain_by_rows(bank)
                else:
                    gain(bank)
            for bank in final_banks(n, FINAL_LAG):
                final_scale(bank)
                if bank == BANKS - 2:
                    store(CHUNKS - 1, 0, 1)
                elif bank == BANKS - 1:
                    store(CHUNKS - 1, 1, 1)
                elif bank % CHUNK_BANKS == CHUNK_BANKS - 1:
                    store(bank // CHUNK_BANKS, 0, CHUNK_HEADS)
            if n == MEAN_STEP_FIRST:
                mean(0)
            for t_tile in t_tile_at(n, MEAN_STEP):
                if t_tile > 0:
                    mean(t_tile)
            for t_tile in t_tile_at(n, STD_STEP):
                std(t_tile)
                split_stats(t_tile)
            for t_tile in t_tile_at(n, STD_STEP + 1):
                inv_std(t_tile)
            for t_tile in t_tile_at(n, ROWS_LAG):
                rows_of_stats(t_tile)
            for t_tile in t_tile_at(n, COPY_LAG):
                copy_rows(t_tile)
            for chunk_no in own_chunks:
                if n == shift_step(chunk_no):
                    shift_and_store(chunk_no)
            if n in X_INTERLEAVE_AT:
                x_interleave(X_INTERLEAVE_AT[n])
            if n in X_QUANTIZE_AT:
                x_quantize(X_QUANTIZE_AT[n])
